import numpy as np
import ml_dtypes


def mxq(x, axis, fmt="e4m3"):
    dtype, down = {"e4m3": (ml_dtypes.float8_e4m3fn, 7), "e5m2": (ml_dtypes.float8_e5m2, 14)}[fmt]
    v = np.moveaxis(np.asarray(x, np.float32).astype(ml_dtypes.bfloat16).astype(np.float64), axis, -1)
    blocks = v.reshape(v.shape[:-1] + (-1, 32))
    amax = np.abs(blocks).max(-1, keepdims=True)
    byte = np.maximum(np.where(amax > 0, np.frexp(amax)[1] - 1 + 127, 0) - down, 1)
    scale = np.exp2(byte - 127.0)
    codes = (blocks / scale).astype(np.float32).astype(dtype).astype(np.float64)
    return np.moveaxis((codes * scale).reshape(v.shape), -1, axis)


WIDE = False


def mx_kscale(k):
    if not WIDE:
        return np.ones(k)
    levels = np.array([20, -20, 10, -10, 0])
    a = np.random.permutation(np.resize(levels, k // 512 * 4)).reshape(k // 512, 4)
    idx = np.arange(k)
    return np.exp2(a[idx // 512, idx % 128 // 32])


BF16 = ml_dtypes.bfloat16


def bf(x):
    return np.asarray(x, np.float32).astype(BF16)


def f64(x):
    return np.asarray(x).astype(np.float64)


B, I, H, P = 512, 128, 512, 2048
C = I + H


def sigmoid(v):
    return 1.0 / (1.0 + np.exp(-v))


def setup_inputs():
    s = mx_kscale(B)[:, None]
    x = np.random.standard_normal((B, I)) * s
    rh = np.random.standard_normal((B, H)) * 0.95 * s
    update = np.random.standard_normal((B, H)) * 0.7
    hidden = 1.5 + np.random.standard_normal((B, H))
    Wn = np.random.standard_normal((H, C)) / np.sqrt(C)
    bn = -0.1 + 0.2 * np.random.standard_normal(H)
    connection_strength = 1.0 + 0.3 * np.random.standard_normal(H)
    connection_decay = 0.4 + 0.2 * np.random.random(1)
    connection_history = 2.0 * np.random.standard_normal(H)
    g = np.random.standard_normal((B, H)) * np.exp2(np.random.randint(-12, 1, (B, 1))) / s
    return {"x": bf(x),
            "rh": bf(rh),
            "update": bf(update),
            "hidden": bf(hidden),
            "Wn": bf(Wn),
            "bn": bf(bn),
            "connection_strength": bf(connection_strength),
            "connection_decay": bf(connection_decay),
            "connection_history": bf(connection_history),
            "grad_out": bf(g)}


def reference(x, rh, update, hidden, Wn, bn, connection_strength, connection_decay, connection_history, grad_out):
    h = f64(hidden)
    activity = np.mean(np.abs(h), axis=0)
    ch = f64(connection_history) * f64(connection_decay) + activity
    cs = f64(connection_strength) * sigmoid(ch)
    gu = f64(grad_out) * f64(update)
    combined_reset = np.concatenate([f64(x), f64(rh)], axis=1)
    prod = mxq(gu, 0, "e5m2").T @ mxq(combined_reset, 0, "e4m3")
    return cs[:, None] * prod

@@ -1,0 +1,210 @@
+from contextlib import ExitStack
+
+import concourse.mybir as mybir
+
+BF16 = mybir.dt.bfloat16
+F32 = mybir.dt.float32
+U32 = mybir.dt.uint32
+U8 = mybir.dt.uint8
+I32 = mybir.dt.int32
+E4M3_X4 = mybir.dt.float8_e4m3fn_x4
+E5M2_X4 = mybir.dt.float8_e5m2_x4
+ACT = mybir.ActivationFunctionType
+ALU = mybir.AluOpType
+
+P = 128
+PACK = 4
+TOKENS = P * PACK
+X_COLS = 128
+H = 512
+C = X_COLS + H
+J_TILES = H // P
+N_PASS = 512
+LOW_COLS = 448
+RUN = 4
+LOAD_PIECES = 2
+WARM_COLS = 256
+
+FLOPS = 2 * TOKENS * H * C
+BYTES = 2 * (TOKENS * X_COLS + 4 * TOKENS * H + 2 * H + 1) + 4 * H * C
+
+
+def token_major(dram):
+    return dram.rearrange("(p t) c -> p t c", t=PACK)
+
+
+def walk_rows(rows):
+    return rows.rearrange("p t (c i) -> p c t i", i=RUN)
+
+
+def walk_grouped(grouped):
+    return grouped.rearrange("p (c i) t -> p c t i", i=RUN)
+
+
+def tile_persistentgrucell_pb_s_kernel(
+    tc,
+    x,
+    rh,
+    update,
+    hidden,
+    Wn,
+    bn,
+    connection_strength,
+    connection_decay,
+    connection_history,
+    grad_out,
+    out,
+):
+    nc = tc.nc
+    with ExitStack() as ctx:
+        keep = ctx.enter_context(tc.tile_pool(name="keep", bufs=1))
+        results = ctx.enter_context(tc.tile_pool(name="results", bufs=J_TILES))
+        banks = ctx.enter_context(tc.psum_pool(name="banks", bufs=3))
+        small_bank = ctx.enter_context(tc.psum_pool(name="small_bank", bufs=1))
+        warm_bank = ctx.enter_context(tc.psum_pool(name="warm_bank", bufs=1))
+        ctx.enter_context(tc.manual_schedule())
+
+        vector_rows = keep.tile([P, 2, H], BF16)
+        decay_col = keep.tile([P, 1], BF16)
+        mean_col = keep.tile([P, 1], BF16)
+        one_col = keep.tile([P, 1], BF16)
+        zero_col = keep.tile([P, 1], F32)
+        nc.vector.memset(vector_rows[:].bitcast(I32), 0)
+        nc.vector.memset(decay_col[:], 0.0)
+        nc.scalar.dma_start(out=vector_rows[0:1, 0, :], in_=connection_history.rearrange("(o j) -> o j", o=1))
+        nc.scalar.dma_start(out=vector_rows[0:1, 1, :], in_=connection_strength.rearrange("(o j) -> o j", o=1))
+        nc.scalar.dma_start(out=decay_col[0:1, :], in_=connection_decay.rearrange("(o j) -> o j", o=1))
+        nc.vector.memset(mean_col[:], 1.0 / TOKENS)
+        nc.vector.memset(one_col[:], 1.0)
+        nc.vector.memset(zero_col[:], 0.0)
+
+        table_warm = keep.tile([P, 1], F32)
+        nc.scalar.activation(out=table_warm[:], in_=zero_col[:], func=ACT.Sigmoid)
+
+        x_rows = keep.tile([P, PACK, X_COLS], BF16)
+        rh_rows = keep.tile([P, PACK, H], BF16)
+        hidden_rows = keep.tile([P, PACK, H], BF16)
+        grad_rows = keep.tile([P, PACK, H], BF16)
+        update_rows = keep.tile([P, PACK, H], BF16)
+        nc.sync.dma_start(out=x_rows[:], in_=token_major(x))
+        nc.sync.dma_start(out=rh_rows[:], in_=token_major(rh))
+        nc.sync.dma_start(out=hidden_rows[:], in_=token_major(hidden))
+        piece_cols = H // LOAD_PIECES
+        for piece in range(LOAD_PIECES):
+            cols = slice(piece * piece_cols, (piece + 1) * piece_cols)
+            nc.sync.dma_start(out=grad_rows[:, :, cols], in_=token_major(grad_out)[:, :, cols])
+            nc.sync.dma_start(out=update_rows[:, :, cols], in_=token_major(update)[:, :, cols])
+
+        for landed in (rh_rows, hidden_rows, grad_rows):
+            unread = warm_bank.tile([P, WARM_COLS], F32)
+            nc.tensor.matmul(
+                out=unread[:],
+                lhsT=landed[:, 0, 0 : 2 * P].bitcast(F32),
+                rhs=rh_rows[:, 1, :].bitcast(F32),
+                start=True,
+                stop=True,
+            )
+
+        joined_grouped = keep.tile([P, C, PACK], BF16, align_bytes=64)
+        joined_codes = keep.tile([P, C], U32, align_bytes=64)
+        joined_scales = keep.tile([P, C], U8, align_bytes=64)
+        nc.vector.tensor_copy(out=walk_grouped(joined_grouped[:, 0:X_COLS, :]), in_=walk_rows(x_rows[:]))
+        nc.vector.tensor_copy(out=walk_grouped(joined_grouped[:, X_COLS:C, :]), in_=walk_rows(rh_rows[:]))
+        for cols in (slice(0, X_COLS), slice(X_COLS, C)):
+            nc.vector.quantize_mx(
+                out=joined_codes[:, cols].bitcast(E4M3_X4),
+                scales=joined_scales[:, cols],
+                in_=joined_grouped[:, cols, :].rearrange("p c t -> p (c t)"),
+            )
+
+        small = small_bank.tile([P, 2, J_TILES], F32)
+        hidden_abs = keep.tile([P, PACK, H], BF16)
+        strength = keep.tile([P, J_TILES], F32)
+        gate = keep.tile([P, J_TILES], F32)
+        cs = keep.tile([P, J_TILES], F32)
+        for jt in range(J_TILES):
+            rows = slice(jt * P, (jt + 1) * P)
+            nc.scalar.activation(out=hidden_abs[:, :, rows], in_=hidden_rows[:, :, rows], func=ACT.Abs)
+            nc.tensor.matmul(
+                out=small[:, 0, jt : jt + 1], lhsT=vector_rows[:, 0, rows], rhs=decay_col[:], start=True, stop=False
+            )
+            for t in range(PACK):
+                nc.tensor.matmul(
+                    out=small[:, 0, jt : jt + 1],
+                    lhsT=hidden_abs[:, t, rows],
+                    rhs=mean_col[:],
+                    start=False,
+                    stop=(t == PACK - 1),
+                )
+        for jt in range(J_TILES):
+            rows = slice(jt * P, (jt + 1) * P)
+            nc.tensor.matmul(
+                out=small[:, 1, jt : jt + 1], lhsT=vector_rows[:, 1, rows], rhs=one_col[:], start=True, stop=True
+            )
+        nc.scalar.activation(out=gate[:], in_=small[:, 0, :], func=ACT.Sigmoid)
+        nc.scalar.copy(out=strength[:], in_=small[:, 1, :])
+        for jt in range(J_TILES):
+            nc.scalar.activation(
+                out=cs[:, jt : jt + 1], in_=gate[:, jt : jt + 1], func=ACT.Copy, scale=strength[:, jt : jt + 1]
+            )
+
+        product_grouped = keep.tile([P, H, PACK], BF16, align_bytes=64)
+        product_codes = keep.tile([P, H], U32, align_bytes=64)
+        product_scales = keep.tile([P, H], U8, align_bytes=64)
+
+        def multiply(jt):
+            rows = slice(jt * P, (jt + 1) * P)
+            nc.vector.tensor_tensor(
+                out=walk_grouped(product_grouped[:, rows, :]),
+                in0=walk_rows(grad_rows[:, :, rows]),
+                in1=walk_rows(update_rows[:, :, rows]),
+                op=ALU.mult,
+            )
+
+        def quantise(jt):
+            rows = slice(jt * P, (jt + 1) * P)
+            nc.vector.quantize_mx(
+                out=product_codes[:, rows].bitcast(E5M2_X4),
+                scales=product_scales[:, rows],
+                in_=product_grouped[:, rows, :].rearrange("p c t -> p (c t)"),
+            )
+
+        def contract_and_store(jt, vector_is_free):
+            rows = slice(jt * P, (jt + 1) * P)
+            low = banks.tile([P, N_PASS], F32)
+            high = banks.tile([P, N_PASS], F32)
+            for bank, first in ((low, 0), (high, C - N_PASS)):
+                nc.tensor.matmul_mx(
+                    out=bank[:],
+                    lhsT=product_codes[:, rows].bitcast(E5M2_X4),
+                    lhsT_scale=product_scales[:, rows],
+                    rhs=joined_codes[:, first : first + N_PASS].bitcast(E4M3_X4),
+                    rhs_scale=joined_scales[:, first : first + N_PASS],
+                    start=True,
+                    stop=True,
+                )
+            result = results.tile([P, C], F32)
+            nc.scalar.activation(out=result[:, 0:LOW_COLS], in_=low[:, 0:LOW_COLS], func=ACT.Copy, scale=cs[:, jt : jt + 1])
+            if vector_is_free:
+                nc.vector.tensor_scalar(
+                    out=result[:, LOW_COLS:C],
+                    in0=high[:, N_PASS - (C - LOW_COLS) : N_PASS],
+                    scalar1=cs[:, jt : jt + 1],
+                    scalar2=None,
+                    op0=ALU.mult,
+                )
+            else:
+                nc.scalar.activation(
+                    out=result[:, LOW_COLS:C], in_=high[:, N_PASS - (C - LOW_COLS) : N_PASS], func=ACT.Copy, scale=cs[:, jt : jt + 1]
+                )
+            nc.sync.dma_start(out=out[rows, :], in_=result[:])
+
+        tiles_in_piece = J_TILES // LOAD_PIECES
+        for piece in range(LOAD_PIECES):
+            tiles = range(piece * tiles_in_piece, (piece + 1) * tiles_in_piece)
+            for jt in tiles:
+                multiply(jt)
+            for jt in tiles:
+                quantise(jt)
+            for jt in tiles:
+                contract_and_store(jt, vector_is_free=(piece == LOAD_PIECES - 1))

@@ -152,12 +152,12 @@ def tile_persistentgrucell_pb_s_kernel(
         product_codes = keep.tile([P, H], U32, align_bytes=64)
         product_scales = keep.tile([P, H], U8, align_bytes=64)
 
-        def multiply(jt):
-            rows = slice(jt * P, (jt + 1) * P)
+        def multiply(first, last):
+            cols = slice(first, last)
             nc.vector.tensor_tensor(
-                out=walk_grouped(product_grouped[:, rows, :]),
-                in0=walk_rows(grad_rows[:, :, rows]),
-                in1=walk_rows(update_rows[:, :, rows]),
+                out=walk_grouped(product_grouped[:, cols, :]),
+                in0=walk_rows(grad_rows[:, :, cols]),
+                in1=walk_rows(update_rows[:, :, cols]),
                 op=ALU.mult,
             )
 
@@ -199,12 +199,13 @@ def tile_persistentgrucell_pb_s_kernel(
                 )
             nc.sync.dma_start(out=out[rows, :], in_=result[:])
 
-        tiles_in_piece = J_TILES // LOAD_PIECES
         for piece in range(LOAD_PIECES):
-            tiles = range(piece * tiles_in_piece, (piece + 1) * tiles_in_piece)
-            for jt in tiles:
-                multiply(jt)
-            for jt in tiles:
-                quantise(jt)
-            for jt in tiles:
+            even, odd = 2 * piece, 2 * piece + 1
+            half = odd * P + P // 2
+            multiply(even * P, odd * P)
+            multiply(odd * P, half)
+            quantise(even)
+            multiply(half, (odd + 1) * P)
+            quantise(odd)
+            for jt in (even, odd):
                 contract_and_store(jt, vector_is_free=(piece == LOAD_PIECES - 1))

@@ -23,6 +23,7 @@ N_PASS = 512
 LOW_COLS = 448
 RUN = 4
 LOAD_PIECES = 2
+SCALAR_RH_COLS = 192
 WARM_COLS = 256
 
 FLOPS = 2 * TOKENS * H * C
@@ -95,7 +96,7 @@ def tile_persistentgrucell_pb_s_kernel(
             nc.sync.dma_start(out=grad_rows[:, :, cols], in_=token_major(grad_out)[:, :, cols])
             nc.sync.dma_start(out=update_rows[:, :, cols], in_=token_major(update)[:, :, cols])
 
-        for landed in (rh_rows, hidden_rows, grad_rows):
+        def warm_up(landed):
             unread = warm_bank.tile([P, WARM_COLS], F32)
             nc.tensor.matmul(
                 out=unread[:],
@@ -105,47 +106,59 @@ def tile_persistentgrucell_pb_s_kernel(
                 stop=True,
             )
 
+        warm_up(rh_rows)
+        warm_up(hidden_rows)
+
         joined_grouped = keep.tile([P, C, PACK], BF16, align_bytes=64)
         joined_codes = keep.tile([P, C], U32, align_bytes=64)
         joined_scales = keep.tile([P, C], U8, align_bytes=64)
-        nc.vector.tensor_copy(out=walk_grouped(joined_grouped[:, 0:X_COLS, :]), in_=walk_rows(x_rows[:]))
-        nc.vector.tensor_copy(out=walk_grouped(joined_grouped[:, X_COLS:C, :]), in_=walk_rows(rh_rows[:]))
-        for cols in (slice(0, X_COLS), slice(X_COLS, C)):
-            nc.vector.quantize_mx(
-                out=joined_codes[:, cols].bitcast(E4M3_X4),
-                scales=joined_scales[:, cols],
-                in_=joined_grouped[:, cols, :].rearrange("p c t -> p (c t)"),
-            )
+        split = X_COLS + SCALAR_RH_COLS
+        nc.scalar.copy(out=walk_grouped(joined_grouped[:, 0:X_COLS, :]), in_=walk_rows(x_rows[:]))
+        nc.scalar.copy(out=walk_grouped(joined_grouped[:, X_COLS:split, :]), in_=walk_rows(rh_rows[:, :, 0:SCALAR_RH_COLS]))
+        nc.vector.tensor_copy(out=walk_grouped(joined_grouped[:, split:C, :]), in_=walk_rows(rh_rows[:, :, SCALAR_RH_COLS:H]))
 
-        small = small_bank.tile([P, 2, J_TILES], F32)
+        small = small_bank.tile([P, J_TILES], F32)
+        strength_bank = warm_bank.tile([P, J_TILES], F32, name="unread")
         hidden_abs = keep.tile([P, PACK, H], BF16)
         strength = keep.tile([P, J_TILES], F32)
         gate = keep.tile([P, J_TILES], F32)
         cs = keep.tile([P, J_TILES], F32)
+        nc.vector.tensor_scalar(
+            out=hidden_abs[:].bitcast(I32),
+            in0=hidden_rows[:].bitcast(I32),
+            scalar1=0x7FFF7FFF,
+            scalar2=None,
+            op0=ALU.bitwise_and,
+        )
         for jt in range(J_TILES):
             rows = slice(jt * P, (jt + 1) * P)
-            nc.scalar.activation(out=hidden_abs[:, :, rows], in_=hidden_rows[:, :, rows], func=ACT.Abs)
             nc.tensor.matmul(
-                out=small[:, 0, jt : jt + 1], lhsT=vector_rows[:, 0, rows], rhs=decay_col[:], start=True, stop=False
+                out=strength_bank[:, jt : jt + 1], lhsT=vector_rows[:, 1, rows], rhs=one_col[:], start=True, stop=True
             )
+        for jt in range(J_TILES):
+            rows = slice(jt * P, (jt + 1) * P)
+            nc.tensor.matmul(out=small[:, jt : jt + 1], lhsT=vector_rows[:, 0, rows], rhs=decay_col[:], start=True, stop=False)
             for t in range(PACK):
                 nc.tensor.matmul(
-                    out=small[:, 0, jt : jt + 1],
+                    out=small[:, jt : jt + 1],
                     lhsT=hidden_abs[:, t, rows],
                     rhs=mean_col[:],
                     start=False,
                     stop=(t == PACK - 1),
                 )
-        for jt in range(J_TILES):
-            rows = slice(jt * P, (jt + 1) * P)
-            nc.tensor.matmul(
-                out=small[:, 1, jt : jt + 1], lhsT=vector_rows[:, 1, rows], rhs=one_col[:], start=True, stop=True
-            )
-        nc.scalar.activation(out=gate[:], in_=small[:, 0, :], func=ACT.Sigmoid)
-        nc.scalar.copy(out=strength[:], in_=small[:, 1, :])
+        nc.scalar.copy(out=strength[:], in_=strength_bank[:])
+        nc.scalar.activation(out=gate[:], in_=small[:], func=ACT.Sigmoid)
         for jt in range(J_TILES):
             nc.scalar.activation(
                 out=cs[:, jt : jt + 1], in_=gate[:, jt : jt + 1], func=ACT.Copy, scale=strength[:, jt : jt + 1]
+            )
+        warm_up(grad_rows)
+
+        for cols in (slice(0, X_COLS), slice(X_COLS, C)):
+            nc.vector.quantize_mx(
+                out=joined_codes[:, cols].bitcast(E4M3_X4),
+                scales=joined_scales[:, cols],
+                in_=joined_grouped[:, cols, :].rearrange("p c t -> p (c t)"),
             )
 
         product_grouped = keep.tile([P, H, PACK], BF16, align_bytes=64)

@@ -20,7 +20,8 @@ H = 512
 C = X_COLS + H
 J_TILES = H // P
 N_PASS = 512
-LOW_COLS = 448
+FIRST_COLS = 448
+SECOND_COLS = C - FIRST_COLS
 RUN = 4
 LOAD_PIECES = 2
 SCALAR_RH_COLS = 192
@@ -87,7 +88,6 @@ def tile_persistentgrucell_pb_s_kernel(
         hidden_rows = keep.tile([P, PACK, H], BF16)
         grad_rows = keep.tile([P, PACK, H], BF16)
         update_rows = keep.tile([P, PACK, H], BF16)
-        nc.sync.dma_start(out=x_rows[:], in_=token_major(x))
         nc.sync.dma_start(out=rh_rows[:], in_=token_major(rh))
         nc.sync.dma_start(out=hidden_rows[:], in_=token_major(hidden))
         piece_cols = H // LOAD_PIECES
@@ -95,6 +95,8 @@ def tile_persistentgrucell_pb_s_kernel(
             cols = slice(piece * piece_cols, (piece + 1) * piece_cols)
             nc.sync.dma_start(out=grad_rows[:, :, cols], in_=token_major(grad_out)[:, :, cols])
             nc.sync.dma_start(out=update_rows[:, :, cols], in_=token_major(update)[:, :, cols])
+            if piece == 0:
+                nc.sync.dma_start(out=x_rows[:], in_=token_major(x))
 
         def warm_up(landed):
             unread = warm_bank.tile([P, WARM_COLS], F32)
@@ -113,8 +115,8 @@ def tile_persistentgrucell_pb_s_kernel(
         joined_codes = keep.tile([P, C], U32, align_bytes=64)
         joined_scales = keep.tile([P, C], U8, align_bytes=64)
         split = X_COLS + SCALAR_RH_COLS
-        nc.scalar.copy(out=walk_grouped(joined_grouped[:, 0:X_COLS, :]), in_=walk_rows(x_rows[:]))
         nc.scalar.copy(out=walk_grouped(joined_grouped[:, X_COLS:split, :]), in_=walk_rows(rh_rows[:, :, 0:SCALAR_RH_COLS]))
+        nc.scalar.copy(out=walk_grouped(joined_grouped[:, 0:X_COLS, :]), in_=walk_rows(x_rows[:]))
         nc.vector.tensor_copy(out=walk_grouped(joined_grouped[:, split:C, :]), in_=walk_rows(rh_rows[:, :, SCALAR_RH_COLS:H]))
 
         small = small_bank.tile([P, J_TILES], F32)
@@ -154,12 +156,14 @@ def tile_persistentgrucell_pb_s_kernel(
             )
         warm_up(grad_rows)
 
-        for cols in (slice(0, X_COLS), slice(X_COLS, C)):
+        def quantise_joined(first, last):
             nc.vector.quantize_mx(
-                out=joined_codes[:, cols].bitcast(E4M3_X4),
-                scales=joined_scales[:, cols],
-                in_=joined_grouped[:, cols, :].rearrange("p c t -> p (c t)"),
+                out=joined_codes[:, first:last].bitcast(E4M3_X4),
+                scales=joined_scales[:, first:last],
+                in_=joined_grouped[:, first:last, :].rearrange("p c t -> p (c t)"),
             )
+
+        quantise_joined(X_COLS, C)
 
         product_grouped = keep.tile([P, H, PACK], BF16, align_bytes=64)
         product_codes = keep.tile([P, H], U32, align_bytes=64)
@@ -184,9 +188,9 @@ def tile_persistentgrucell_pb_s_kernel(
 
         def contract_and_store(jt, vector_is_free):
             rows = slice(jt * P, (jt + 1) * P)
-            low = banks.tile([P, N_PASS], F32)
-            high = banks.tile([P, N_PASS], F32)
-            for bank, first in ((low, 0), (high, C - N_PASS)):
+            rh_bank = banks.tile([P, N_PASS], F32)
+            x_bank = banks.tile([P, N_PASS], F32)
+            for bank, first in ((rh_bank, C - N_PASS), (x_bank, 0)):
                 nc.tensor.matmul_mx(
                     out=bank[:],
                     lhsT=product_codes[:, rows].bitcast(E5M2_X4),
@@ -197,19 +201,19 @@ def tile_persistentgrucell_pb_s_kernel(
                     stop=True,
                 )
             result = results.tile([P, C], F32)
-            nc.scalar.activation(out=result[:, 0:LOW_COLS], in_=low[:, 0:LOW_COLS], func=ACT.Copy, scale=cs[:, jt : jt + 1])
+            nc.scalar.activation(
+                out=result[:, SECOND_COLS:C], in_=rh_bank[:, N_PASS - FIRST_COLS : N_PASS], func=ACT.Copy, scale=cs[:, jt : jt + 1]
+            )
             if vector_is_free:
                 nc.vector.tensor_scalar(
-                    out=result[:, LOW_COLS:C],
-                    in0=high[:, N_PASS - (C - LOW_COLS) : N_PASS],
+                    out=result[:, 0:SECOND_COLS],
+                    in0=x_bank[:, 0:SECOND_COLS],
                     scalar1=cs[:, jt : jt + 1],
                     scalar2=None,
                     op0=ALU.mult,
                 )
             else:
-                nc.scalar.activation(
-                    out=result[:, LOW_COLS:C], in_=high[:, N_PASS - (C - LOW_COLS) : N_PASS], func=ACT.Copy, scale=cs[:, jt : jt + 1]
-                )
+                nc.scalar.activation(out=result[:, 0:SECOND_COLS], in_=x_bank[:, 0:SECOND_COLS], func=ACT.Copy, scale=cs[:, jt : jt + 1])
             nc.sync.dma_start(out=out[rows, :], in_=result[:])
 
         for piece in range(LOAD_PIECES):
@@ -219,6 +223,8 @@ def tile_persistentgrucell_pb_s_kernel(
             multiply(odd * P, half)
             quantise(even)
             multiply(half, (odd + 1) * P)
+            if piece == 0:
+                quantise_joined(0, X_COLS)
             quantise(odd)
             for jt in (even, odd):
                 contract_and_store(jt, vector_is_free=(piece == LOAD_PIECES - 1))

@@ -116,7 +116,6 @@ def tile_persistentgrucell_pb_s_kernel(
         joined_scales = keep.tile([P, C], U8, align_bytes=64)
         split = X_COLS + SCALAR_RH_COLS
         nc.scalar.copy(out=walk_grouped(joined_grouped[:, X_COLS:split, :]), in_=walk_rows(rh_rows[:, :, 0:SCALAR_RH_COLS]))
-        nc.scalar.copy(out=walk_grouped(joined_grouped[:, 0:X_COLS, :]), in_=walk_rows(x_rows[:]))
         nc.vector.tensor_copy(out=walk_grouped(joined_grouped[:, split:C, :]), in_=walk_rows(rh_rows[:, :, SCALAR_RH_COLS:H]))
 
         small = small_bank.tile([P, J_TILES], F32)
@@ -137,6 +136,8 @@ def tile_persistentgrucell_pb_s_kernel(
             nc.tensor.matmul(
                 out=strength_bank[:, jt : jt + 1], lhsT=vector_rows[:, 1, rows], rhs=one_col[:], start=True, stop=True
             )
+        nc.scalar.copy(out=strength[:], in_=strength_bank[:])
+        nc.scalar.copy(out=walk_grouped(joined_grouped[:, 0:X_COLS, :]), in_=walk_rows(x_rows[:]))
         for jt in range(J_TILES):
             rows = slice(jt * P, (jt + 1) * P)
             nc.tensor.matmul(out=small[:, jt : jt + 1], lhsT=vector_rows[:, 0, rows], rhs=decay_col[:], start=True, stop=False)
@@ -148,7 +149,6 @@ def tile_persistentgrucell_pb_s_kernel(
                     start=False,
                     stop=(t == PACK - 1),
                 )
-        nc.scalar.copy(out=strength[:], in_=strength_bank[:])
         nc.scalar.activation(out=gate[:], in_=small[:], func=ACT.Sigmoid)
         for jt in range(J_TILES):
             nc.scalar.activation(

from contextlib import ExitStack

import concourse.mybir as mybir

BF16 = mybir.dt.bfloat16
F32 = mybir.dt.float32
U32 = mybir.dt.uint32
U8 = mybir.dt.uint8
I32 = mybir.dt.int32
E4M3_X4 = mybir.dt.float8_e4m3fn_x4
E5M2_X4 = mybir.dt.float8_e5m2_x4
ACT = mybir.ActivationFunctionType
ALU = mybir.AluOpType

P = 128
PACK = 4
TOKENS = P * PACK
X_COLS = 128
H = 512
C = X_COLS + H
J_TILES = H // P
N_PASS = 512
FIRST_COLS = 448
SECOND_COLS = C - FIRST_COLS
RUN = 4
LOAD_PIECES = 2
SCALAR_RH_COLS = 192
WARM_COLS = 256

FLOPS = 2 * TOKENS * H * C
BYTES = 2 * (TOKENS * X_COLS + 4 * TOKENS * H + 2 * H + 1) + 4 * H * C


def token_major(dram):
    return dram.rearrange("(p t) c -> p t c", t=PACK)


def walk_rows(rows):
    return rows.rearrange("p t (c i) -> p c t i", i=RUN)


def walk_grouped(grouped):
    return grouped.rearrange("p (c i) t -> p c t i", i=RUN)


def tile_persistentgrucell_pb_s_kernel(
    tc,
    x,
    rh,
    update,
    hidden,
    Wn,
    bn,
    connection_strength,
    connection_decay,
    connection_history,
    grad_out,
    out,
):
    nc = tc.nc
    with ExitStack() as ctx:
        keep = ctx.enter_context(tc.tile_pool(name="keep", bufs=1))
        results = ctx.enter_context(tc.tile_pool(name="results", bufs=J_TILES))
        banks = ctx.enter_context(tc.psum_pool(name="banks", bufs=3))
        small_bank = ctx.enter_context(tc.psum_pool(name="small_bank", bufs=1))
        warm_bank = ctx.enter_context(tc.psum_pool(name="warm_bank", bufs=1))
        ctx.enter_context(tc.manual_schedule())

        vector_rows = keep.tile([P, 2, H], BF16)
        decay_col = keep.tile([P, 1], BF16)
        mean_col = keep.tile([P, 1], BF16)
        one_col = keep.tile([P, 1], BF16)
        zero_col = keep.tile([P, 1], F32)
        nc.vector.memset(vector_rows[:].bitcast(I32), 0)
        nc.vector.memset(decay_col[:], 0.0)
        nc.scalar.dma_start(out=vector_rows[0:1, 0, :], in_=connection_history.rearrange("(o j) -> o j", o=1))
        nc.scalar.dma_start(out=vector_rows[0:1, 1, :], in_=connection_strength.rearrange("(o j) -> o j", o=1))
        nc.scalar.dma_start(out=decay_col[0:1, :], in_=connection_decay.rearrange("(o j) -> o j", o=1))
        nc.vector.memset(mean_col[:], 1.0 / TOKENS)
        nc.vector.memset(one_col[:], 1.0)
        nc.vector.memset(zero_col[:], 0.0)

        table_warm = keep.tile([P, 1], F32)
        nc.scalar.activation(out=table_warm[:], in_=zero_col[:], func=ACT.Sigmoid)

        x_rows = keep.tile([P, PACK, X_COLS], BF16)
        rh_rows = keep.tile([P, PACK, H], BF16)
        hidden_rows = keep.tile([P, PACK, H], BF16)
        grad_rows = keep.tile([P, PACK, H], BF16)
        update_rows = keep.tile([P, PACK, H], BF16)
        nc.sync.dma_start(out=rh_rows[:], in_=token_major(rh))
        nc.sync.dma_start(out=hidden_rows[:], in_=token_major(hidden))
        piece_cols = H // LOAD_PIECES
        for piece in range(LOAD_PIECES):
            cols = slice(piece * piece_cols, (piece + 1) * piece_cols)
            nc.sync.dma_start(out=grad_rows[:, :, cols], in_=token_major(grad_out)[:, :, cols])
            nc.sync.dma_start(out=update_rows[:, :, cols], in_=token_major(update)[:, :, cols])
            if piece == 0:
                nc.sync.dma_start(out=x_rows[:], in_=token_major(x))

        def warm_up(landed):
            unread = warm_bank.tile([P, WARM_COLS], F32)
            nc.tensor.matmul(
                out=unread[:],
                lhsT=landed[:, 0, 0 : 2 * P].bitcast(F32),
                rhs=rh_rows[:, 1, :].bitcast(F32),
                start=True,
                stop=True,
            )

        warm_up(rh_rows)
        warm_up(hidden_rows)

        joined_grouped = keep.tile([P, C, PACK], BF16, align_bytes=64)
        joined_codes = keep.tile([P, C], U32, align_bytes=64)
        joined_scales = keep.tile([P, C], U8, align_bytes=64)
        split = X_COLS + SCALAR_RH_COLS
        nc.scalar.copy(out=walk_grouped(joined_grouped[:, X_COLS:split, :]), in_=walk_rows(rh_rows[:, :, 0:SCALAR_RH_COLS]))
        nc.vector.tensor_copy(out=walk_grouped(joined_grouped[:, split:C, :]), in_=walk_rows(rh_rows[:, :, SCALAR_RH_COLS:H]))

        small = small_bank.tile([P, J_TILES], F32)
        strength_bank = warm_bank.tile([P, J_TILES], F32, name="unread")
        hidden_abs = keep.tile([P, PACK, H], BF16)
        strength = keep.tile([P, J_TILES], F32)
        gate = keep.tile([P, J_TILES], F32)
        cs = keep.tile([P, J_TILES], F32)
        nc.vector.tensor_scalar(
            out=hidden_abs[:].bitcast(I32),
            in0=hidden_rows[:].bitcast(I32),
            scalar1=0x7FFF7FFF,
            scalar2=None,
            op0=ALU.bitwise_and,
        )
        for jt in range(J_TILES):
            rows = slice(jt * P, (jt + 1) * P)
            nc.tensor.matmul(
                out=strength_bank[:, jt : jt + 1], lhsT=vector_rows[:, 1, rows], rhs=one_col[:], start=True, stop=True
            )
        nc.scalar.copy(out=strength[:], in_=strength_bank[:])
        nc.scalar.copy(out=walk_grouped(joined_grouped[:, 0:X_COLS, :]), in_=walk_rows(x_rows[:]))
        for jt in range(J_TILES):
            rows = slice(jt * P, (jt + 1) * P)
            nc.tensor.matmul(out=small[:, jt : jt + 1], lhsT=vector_rows[:, 0, rows], rhs=decay_col[:], start=True, stop=False)
            for t in range(PACK):
                nc.tensor.matmul(
                    out=small[:, jt : jt + 1],
                    lhsT=hidden_abs[:, t, rows],
                    rhs=mean_col[:],
                    start=False,
                    stop=(t == PACK - 1),
                )
        nc.scalar.activation(out=gate[:], in_=small[:], func=ACT.Sigmoid)
        for jt in range(J_TILES):
            nc.scalar.activation(
                out=cs[:, jt : jt + 1], in_=gate[:, jt : jt + 1], func=ACT.Copy, scale=strength[:, jt : jt + 1]
            )
        warm_up(grad_rows)

        def quantise_joined(first, last):
            nc.vector.quantize_mx(
                out=joined_codes[:, first:last].bitcast(E4M3_X4),
                scales=joined_scales[:, first:last],
                in_=joined_grouped[:, first:last, :].rearrange("p c t -> p (c t)"),
            )

        quantise_joined(X_COLS, C)

        product_grouped = keep.tile([P, H, PACK], BF16, align_bytes=64)
        product_codes = keep.tile([P, H], U32, align_bytes=64)
        product_scales = keep.tile([P, H], U8, align_bytes=64)

        def multiply(first, last):
            cols = slice(first, last)
            nc.vector.tensor_tensor(
                out=walk_grouped(product_grouped[:, cols, :]),
                in0=walk_rows(grad_rows[:, :, cols]),
                in1=walk_rows(update_rows[:, :, cols]),
                op=ALU.mult,
            )

        def quantise(jt):
            rows = slice(jt * P, (jt + 1) * P)
            nc.vector.quantize_mx(
                out=product_codes[:, rows].bitcast(E5M2_X4),
                scales=product_scales[:, rows],
                in_=product_grouped[:, rows, :].rearrange("p c t -> p (c t)"),
            )

        def contract_and_store(jt, vector_is_free):
            rows = slice(jt * P, (jt + 1) * P)
            rh_bank = banks.tile([P, N_PASS], F32)
            x_bank = banks.tile([P, N_PASS], F32)
            for bank, first in ((rh_bank, C - N_PASS), (x_bank, 0)):
                nc.tensor.matmul_mx(
                    out=bank[:],
                    lhsT=product_codes[:, rows].bitcast(E5M2_X4),
                    lhsT_scale=product_scales[:, rows],
                    rhs=joined_codes[:, first : first + N_PASS].bitcast(E4M3_X4),
                    rhs_scale=joined_scales[:, first : first + N_PASS],
                    start=True,
                    stop=True,
                )
            result = results.tile([P, C], F32)
            nc.scalar.activation(
                out=result[:, SECOND_COLS:C], in_=rh_bank[:, N_PASS - FIRST_COLS : N_PASS], func=ACT.Copy, scale=cs[:, jt : jt + 1]
            )
            if vector_is_free:
                nc.vector.tensor_scalar(
                    out=result[:, 0:SECOND_COLS],
                    in0=x_bank[:, 0:SECOND_COLS],
                    scalar1=cs[:, jt : jt + 1],
                    scalar2=None,
                    op0=ALU.mult,
                )
            else:
                nc.scalar.activation(out=result[:, 0:SECOND_COLS], in_=x_bank[:, 0:SECOND_COLS], func=ACT.Copy, scale=cs[:, jt : jt + 1])
            nc.sync.dma_start(out=out[rows, :], in_=result[:])

        for piece in range(LOAD_PIECES):
            even, odd = 2 * piece, 2 * piece + 1
            half = odd * P + P // 2
            multiply(even * P, odd * P)
            multiply(odd * P, half)
            quantise(even)
            multiply(half, (odd + 1) * P)
            if piece == 0:
                quantise_joined(0, X_COLS)
            quantise(odd)
            for jt in (even, odd):
                contract_and_store(jt, vector_is_free=(piece == LOAD_PIECES - 1))
